import numpy as np
import ml_dtypes


def mxq(x, axis, fmt="e4m3"):
    dtype, down = {"e4m3": (ml_dtypes.float8_e4m3fn, 7), "e5m2": (ml_dtypes.float8_e5m2, 14)}[fmt]
    v = np.moveaxis(np.asarray(x, np.float32).astype(ml_dtypes.bfloat16).astype(np.float64), axis, -1)
    blocks = v.reshape(v.shape[:-1] + (-1, 32))
    amax = np.abs(blocks).max(-1, keepdims=True)
    byte = np.maximum(np.where(amax > 0, np.frexp(amax)[1] - 1 + 127, 0) - down, 1)
    scale = np.exp2(byte - 127.0)
    codes = (blocks / scale).astype(np.float32).astype(dtype).astype(np.float64)
    return np.moveaxis((codes * scale).reshape(v.shape), -1, axis)


WIDE = False


def mx_kscale(k):
    if not WIDE:
        return np.ones(k)
    levels = np.array([10, -10, 5, -5, 0])
    if k % 512:
        return np.exp2(np.random.permutation(np.resize(levels, k // 32))).repeat(32)
    a = np.empty((k // 512, 16))
    for p in range(k // 512):
        a[p, :8] = np.random.permutation(np.resize(levels, 8))
        for g in range(8):
            far = levels[np.abs(levels - a[p, g]) >= 10]
            a[p, g + 8] = far[np.random.randint(len(far))]
    return np.exp2(a.ravel()).repeat(32)


BF16 = ml_dtypes.bfloat16


def bf(x):
    return np.asarray(x, np.float32).astype(BF16)


def f64(x):
    return np.asarray(x).astype(np.float64)


B, A, E, P, R = 512, 8, 512, 512, 512


def setup_inputs():
    s = mx_kscale(B)
    u = mx_kscale(P)
    a0 = bf(np.random.standard_normal((B, A, R)))
    w0 = bf(np.random.standard_normal((A, R, P)) / np.sqrt(R))
    sw = bf(1.0 + 0.3 * np.random.standard_normal((1, A, 1)))
    g = bf(np.random.standard_normal((B, P)) * np.exp2(np.random.randint(-6, 1, (B, 1))) * 4.0 / s[:, None] * u)
    proj = (f64(a0).transpose(1, 0, 2) @ f64(w0)).transpose(1, 0, 2)
    return {
        "attr_rep": bf(f64(a0) * s[:, None, None]),
        "bwd_proj": bf(f64(w0) / u),
        "self_weighted": sw,
        "proj": np.asarray(proj, np.float32),
        "grad_out": g,
    }


def reference(attr_rep, bwd_proj, self_weighted, proj, grad_out):
    mask = np.where(f64(proj) > 0.0, 1.0, 0.0)
    dz = f64(grad_out)[:, None, :] * f64(self_weighted) * mask
    dza = dz.transpose(1, 0, 2)
    wq = mxq(f64(bwd_proj), 2, "e4m3")
    dx = (mxq(dza, 2, "e5m2") @ wq.transpose(0, 2, 1)).transpose(1, 0, 2)
    xa = f64(attr_rep).transpose(1, 2, 0)
    dw = mxq(xa, 2, "e4m3") @ mxq(dza, 1, "e5m2")
    return dx, dw

@@ -1,0 +1,219 @@
+from contextlib import ExitStack
+
+import concourse.mybir as mybir
+from concourse.masks import make_identity
+
+FLOPS = 2 * 2 * 8 * 512 * 512 * 512
+
+F32 = mybir.dt.float32
+BF16 = mybir.dt.bfloat16
+U32 = mybir.dt.uint32
+U8 = mybir.dt.uint8
+E4 = mybir.dt.float8_e4m3fn_x4
+E5 = mybir.dt.float8_e5m2_x4
+ALU = mybir.AluOpType
+
+P = 128
+A = 8
+W = 512
+
+
+def tile_attributegnn_pb_v_kernel(tc, attr_rep, bwd_proj, self_weighted, proj, grad_out, out_0, out_1):
+    nc = tc.nc
+
+    proj_v = proj.rearrange("(p j) a w -> p j a w", j=4)
+    x_v = attr_rep.rearrange("(p j) a r -> p j a r", j=4)
+    g_v = grad_out.rearrange("(p j) w -> p j w", j=4)
+    w_v = bwd_proj.rearrange("a (m t) p -> m a t p", t=4)
+    o0_v = out_0.rearrange("(m j) a r -> m j a r", j=4)
+    o1_v = out_1.rearrange("a (m t) p -> m a t p", t=4)
+
+    with ExitStack() as ctx:
+        const = ctx.enter_context(tc.tile_pool(name="const", bufs=1))
+        sb = ctx.enter_context(tc.tile_pool(name="sb", bufs=2))
+        psum = ctx.enter_context(tc.psum_pool(name="psum", bufs=2))
+        ctx.enter_context(tc.manual_schedule())
+
+        pt = {}
+        xt = {}
+        wt = {}
+        st = {}
+
+        def alloc_pair(k):
+            pt[k] = sb.tile([P, 4, 2, W], F32, name="pt", tag="pt", bufs=3)
+            xt[k] = sb.tile([P, 4, 2, W], BF16, name="xt", tag="xt", bufs=3)
+            wt[k] = sb.tile([P, 2, 4, W], BF16, name="wt", tag="wt", bufs=3)
+
+        def load_pair(k):
+            alloc_pair(k)
+            nc.sync.dma_start(out=pt[k][:], in_=proj_v[:, :, 2 * k : 2 * k + 2, :])
+            nc.sync.dma_start(out=wt[k][:], in_=w_v[:, 2 * k : 2 * k + 2])
+            nc.sync.dma_start(out=xt[k][:], in_=x_v[:, :, 2 * k : 2 * k + 2, :])
+
+        zrow = const.tile([P, 32], BF16, name="zrow")
+        ones = const.tile([P, P], BF16, name="ones")
+        warm = const.tile([P, 1], BF16, name="warm")
+        ident = const.tile([P, P], F32, name="ident")
+        sw_sb = const.tile([P, 32], F32, name="sw_sb")
+        g_sb = const.tile([P, 4, W], BF16, name="g_sb")
+        nc.vector.memset(zrow[:], 0.0)
+        nc.vector.memset(ones[:], 1.0)
+        nc.sync.dma_start(out=zrow[0:1, 0:A], in_=self_weighted.rearrange("o a i -> o (a i)"))
+        alloc_pair(0)
+        nc.sync.dma_start(out=pt[0][:, :, 0, :], in_=proj_v[:, :, 0, :])
+        nc.sync.dma_start(out=g_sb[:], in_=g_v)
+        nc.sync.dma_start(out=xt[0][:, :, 0, :], in_=x_v[:, :, 0, :])
+        nc.sync.dma_start(out=wt[0][:, 0], in_=w_v[:, 0])
+        nc.sync.dma_start(out=pt[0][:, :, 1, :], in_=proj_v[:, :, 1, :])
+        nc.sync.dma_start(out=xt[0][:, :, 1, :], in_=x_v[:, :, 1, :])
+        nc.sync.dma_start(out=wt[0][:, 1], in_=w_v[:, 1])
+        load_pair(1)
+        load_pair(2)
+        nc.scalar.copy(out=warm[:], in_=ones[:, 0:1])
+        make_identity(nc, ident[:])
+        sw_ps = psum.tile([P, W], F32, name="sw_ps", tag="tw", bufs=2)
+        nc.tensor.matmul(out=sw_ps[:, 0:32], lhsT=ones[:], rhs=zrow[:], start=True, stop=True)
+        nc.vector.tensor_copy(out=sw_sb[:], in_=sw_ps[:, 0:32])
+
+        def quant(src, fmt, key, u):
+            codes = sb.tile([P, W], U32, name=key + "c", tag=key + "c", bufs=2, align_bytes=64)
+            scales = sb.tile([P, W], U8, name=key + "s", tag=key + "s", bufs=2, align_bytes=64)
+            nc.vector.quantize_mx(out=codes[:].bitcast(fmt), scales=scales[:], in_=src[:].rearrange("p c k -> p (c k)"))
+            st[(key, u)] = (codes, scales)
+
+        def transposes(words, tag):
+            banks = []
+            for h in range(2):
+                bank = psum.tile([P, W], F32, name=tag, tag=tag, bufs=2)
+                bv = bank[:].rearrange("p (e n) -> p e n", e=2)
+                for s in range(2):
+                    blk = 2 * h + s
+                    for e in range(2):
+                        nc.tensor.transpose(bv[:, e, P * s : P * s + P], words[:, 256 * blk + e : 256 * (blk + 1) : 2], ident[:])
+                banks.append(bank)
+            return banks
+
+        def regroup(banks, tag):
+            grouped = sb.tile([P, W, 4], BF16, name=tag, tag=tag, bufs=2, align_bytes=64)
+            gw = grouped[:].rearrange("p n k -> p (n k)").bitcast(F32)
+            for h in range(2):
+                nc.scalar.copy(
+                    out=gw[:, 512 * h : 512 * h + 512].rearrange("p (n e) -> p n e", e=2),
+                    in_=banks[h][:].rearrange("p (e n) -> p n e", e=2),
+                )
+            return grouped
+
+        def v1(u):
+            msw = sb.tile([P, 4, W], BF16, name="msw", tag="msw", bufs=2)
+            nc.vector.tensor_scalar(out=msw[:], in0=pt[u // 2][:, :, u % 2, :], scalar1=0.0, scalar2=sw_sb[:, u : u + 1], op0=ALU.is_gt, op1=ALU.mult)
+            st[("msw", u)] = msw
+
+        def v2(u):
+            dz = sb.tile([P, 4, W], BF16, name="dz", tag="dz", bufs=2)
+            nc.vector.tensor_tensor(out=dz[:], in0=st[("msw", u)][:], in1=g_sb[:], op=ALU.mult)
+            st[("dz", u)] = dz
+
+        def v3(u):
+            dzb = sb.tile([P, W, 4], BF16, name="dzb", tag="dzb", bufs=2, align_bytes=64)
+            nc.vector.tensor_copy(out=dzb[:], in_=st[("dz", u)][:].rearrange("p j w -> p w j"))
+            st[("dzb", u)] = dzb
+
+        def v4(u):
+            xg = sb.tile([P, W, 4], BF16, name="xg", tag="xg", bufs=2, align_bytes=64)
+            nc.vector.tensor_copy(
+                out=xg[:].rearrange("p (t m) j -> p t m j", t=4),
+                in_=xt[u // 2][:, :, u % 2, :].rearrange("p j (m t) -> p t m j", t=4),
+            )
+            st[("xg", u)] = xg
+
+        def t1(u):
+            st[("wb", u)] = transposes(wt[u // 2][:, u % 2].rearrange("p t w -> p (t w)").bitcast(F32), "tw")
+
+        def s1(u):
+            st[("wg", u)] = regroup(st[("wb", u)], "wg")
+
+        def t2(u):
+            st[("db", u)] = transposes(st[("dz", u)][:].rearrange("p j w -> p (j w)").bitcast(F32), "td")
+
+        def s2(u):
+            st[("dg", u)] = regroup(st[("db", u)], "dg")
+
+        def mms(lhs, lfmt, rhs, rfmt, tags):
+            accs = []
+            for i in range(4):
+                acc = psum.tile([P, W], F32, name=tags[i], tag=tags[i], bufs=(4 if tags[i] == "acc" else 2))
+                nc.tensor.matmul_mx(
+                    out=acc[:],
+                    lhsT=lhs[0][:, P * i : P * i + P].bitcast(lfmt),
+                    lhsT_scale=lhs[1][:, P * i : P * i + P],
+                    rhs=rhs[0][:].bitcast(rfmt),
+                    rhs_scale=rhs[1][:],
+                    start=True,
+                    stop=True,
+                )
+                accs.append(acc)
+            return accs
+
+        def t3(u):
+            st[("a1", u)] = mms(st[("x", u)], E4, st[("b", u)], E5, ["acc"] * 4)
+
+        def t4(u):
+            tags = ["acc"] * 4 if u < A - 1 else ["tw", "tw", "td", "td"]
+            st[("a0", u)] = mms(st[("d", u)], E5, st[("w", u)], E4, tags)
+
+        def s3(u):
+            o1 = sb.tile([P, 4, W], F32, name="o1", tag="o1", bufs=3)
+            last = u == A - 1
+            for i in range(4):
+                nc.scalar.copy(out=o1[:, i, :], in_=st[("a1", u)][i][:])
+                if last and i % 2 == 1:
+                    nc.scalar.dma_start(out=o1_v[:, u, i - 1 : i + 1], in_=o1[:, i - 1 : i + 1, :])
+            if not last:
+                nc.scalar.dma_start(out=o1_v[:, u], in_=o1[:])
+
+        def s4(u):
+            if u % 2 == 0:
+                st[("o0", u // 2)] = sb.tile([P, 4, 2, W], F32, name="o0", tag="o0", bufs=2)
+            o0 = st[("o0", u // 2)]
+            last = u == A - 1
+            for j in range(4):
+                dst = o0[:, j, u % 2, :].rearrange("p (m t) -> p m t", t=4)
+                src = st[("a0", u)][j][:].rearrange("p (t m) -> p m t", t=4)
+                if last:
+                    nc.vector.tensor_copy(out=dst, in_=src)
+                    if j % 2 == 1:
+                        nc.sync.dma_start(out=o0_v[:, j - 1 : j + 1, u, :], in_=o0[:, j - 1 : j + 1, 1, :])
+                else:
+                    nc.scalar.copy(out=dst, in_=src)
+            if u == A - 2:
+                nc.scalar.dma_start(out=o0_v[:, :, u, :], in_=o0[:, :, 0, :])
+            elif u % 2 == 1 and not last:
+                nc.scalar.dma_start(out=o0_v[:, :, u - 1 : u + 1, :], in_=o0[:])
+
+        t1(0)
+        s1(0)
+        for u in range(A):
+            v1(u)
+            if u > 0:
+                quant(st[("dg", u - 1)], E5, "d", u - 1)
+                t4(u - 1)
+                s4(u - 1)
+            v2(u)
+            t2(u)
+            if u + 1 < A:
+                t1(u + 1)
+            s2(u)
+            if u + 1 < A:
+                s1(u + 1)
+            v4(u)
+            v3(u)
+            quant(st[("wg", u)], E4, "w", u)
+            quant(st[("xg", u)], E4, "x", u)
+            quant(st[("dzb", u)], E5, "b", u)
+            if u == 1:
+                load_pair(3)
+            t3(u)
+            s3(u)
+        quant(st[("dg", A - 1)], E5, "d", A - 1)
+        t4(A - 1)
+        s4(A - 1)

@@ -40,9 +40,9 @@ def tile_attributegnn_pb_v_kernel(tc, attr_rep, bwd_proj, self_weighted, proj, g
         st = {}
 
         def alloc_pair(k):
-            pt[k] = sb.tile([P, 4, 2, W], F32, name="pt", tag="pt", bufs=3)
-            xt[k] = sb.tile([P, 4, 2, W], BF16, name="xt", tag="xt", bufs=3)
-            wt[k] = sb.tile([P, 2, 4, W], BF16, name="wt", tag="wt", bufs=3)
+            pt[k] = sb.tile([P, 4, 2, W], F32, name="pt", tag="big", bufs=5)
+            xt[k] = sb.tile([P, 4, 2, W], BF16, name="xt", tag="mid", bufs=10)
+            wt[k] = sb.tile([P, 2, 4, W], BF16, name="wt", tag="mid", bufs=10)
 
         def load_pair(k):
             alloc_pair(k)
@@ -69,6 +69,7 @@ def tile_attributegnn_pb_v_kernel(tc, attr_rep, bwd_proj, self_weighted, proj, g
         nc.sync.dma_start(out=wt[0][:, 1], in_=w_v[:, 1])
         load_pair(1)
         load_pair(2)
+        load_pair(3)
         nc.scalar.copy(out=warm[:], in_=ones[:, 0:1])
         make_identity(nc, ident[:])
         sw_ps = psum.tile([P, W], F32, name="sw_ps", tag="tw", bufs=2)
@@ -162,18 +163,18 @@ def tile_attributegnn_pb_v_kernel(tc, attr_rep, bwd_proj, self_weighted, proj, g
             st[("a0", u)] = mms(st[("d", u)], E5, st[("w", u)], E4, tags)
 
         def s3(u):
-            o1 = sb.tile([P, 4, W], F32, name="o1", tag="o1", bufs=3)
+            o1 = sb.tile([P, 4, W], F32, name="o1", tag="mid", bufs=10)
             last = u == A - 1
             for i in range(4):
                 nc.scalar.copy(out=o1[:, i, :], in_=st[("a1", u)][i][:])
                 if last and i % 2 == 1:
-                    nc.scalar.dma_start(out=o1_v[:, u, i - 1 : i + 1], in_=o1[:, i - 1 : i + 1, :])
+                    nc.sync.dma_start(out=o1_v[:, u, i - 1 : i + 1], in_=o1[:, i - 1 : i + 1, :])
             if not last:
-                nc.scalar.dma_start(out=o1_v[:, u], in_=o1[:])
+                nc.sync.dma_start(out=o1_v[:, u], in_=o1[:])
 
         def s4(u):
             if u % 2 == 0:
-                st[("o0", u // 2)] = sb.tile([P, 4, 2, W], F32, name="o0", tag="o0", bufs=2)
+                st[("o0", u // 2)] = sb.tile([P, 4, 2, W], F32, name="o0", tag="big", bufs=5)
             o0 = st[("o0", u // 2)]
             last = u == A - 1
             for j in range(4):
@@ -186,9 +187,9 @@ def tile_attributegnn_pb_v_kernel(tc, attr_rep, bwd_proj, self_weighted, proj, g
                 else:
                     nc.scalar.copy(out=dst, in_=src)
             if u == A - 2:
-                nc.scalar.dma_start(out=o0_v[:, :, u, :], in_=o0[:, :, 0, :])
+                nc.sync.dma_start(out=o0_v[:, :, u, :], in_=o0[:, :, 0, :])
             elif u % 2 == 1 and not last:
-                nc.scalar.dma_start(out=o0_v[:, :, u - 1 : u + 1, :], in_=o0[:])
+                nc.sync.dma_start(out=o0_v[:, :, u - 1 : u + 1, :], in_=o0[:])
 
         t1(0)
         s1(0)
@@ -210,8 +211,6 @@ def tile_attributegnn_pb_v_kernel(tc, attr_rep, bwd_proj, self_weighted, proj, g
             quant(st[("wg", u)], E4, "w", u)
             quant(st[("xg", u)], E4, "x", u)
             quant(st[("dzb", u)], E5, "b", u)
-            if u == 1:
-                load_pair(3)
             t3(u)
             s3(u)
         quant(st[("dg", A - 1)], E5, "d", A - 1)

@@ -16,6 +16,7 @@ ALU = mybir.AluOpType
 P = 128
 A = 8
 W = 512
+NWARM = 6
 
 
 def tile_attributegnn_pb_v_kernel(tc, attr_rep, bwd_proj, self_weighted, proj, grad_out, out_0, out_1):
@@ -139,10 +140,30 @@ def tile_attributegnn_pb_v_kernel(tc, attr_rep, bwd_proj, self_weighted, proj, g
         def s2(u):
             st[("dg", u)] = regroup(st[("db", u)], "dg")
 
-        def mms(lhs, lfmt, rhs, rfmt, tags):
+        def keep_warm(u):
             accs = []
             for i in range(4):
-                acc = psum.tile([P, W], F32, name=tags[i], tag=tags[i], bufs=(4 if tags[i] == "acc" else 2))
+                acc = psum.tile([P, W], F32, name="acc", tag="acc", bufs=4)
+                accs.append(acc)
+            for i in range(NWARM if u > 0 else 0):
+                nc.tensor.matmul_mx(
+                    out=accs[i % 4][:],
+                    lhsT=st[("d", u - 1)][0][:, 0:P].bitcast(E5),
+                    lhsT_scale=st[("d", u - 1)][1][:, 0:P],
+                    rhs=st[("w", u - 1)][0][:].bitcast(E4),
+                    rhs_scale=st[("w", u - 1)][1][:],
+                    start=True,
+                    stop=True,
+                )
+            st[("pre", u)] = accs
+
+        def mms(lhs, lfmt, rhs, rfmt, tags, pre):
+            accs = []
+            for i in range(4):
+                if pre is None:
+                    acc = psum.tile([P, W], F32, name=tags[i], tag=tags[i], bufs=(4 if tags[i] == "acc" else 2))
+                else:
+                    acc = pre[i]
                 nc.tensor.matmul_mx(
                     out=acc[:],
                     lhsT=lhs[0][:, P * i : P * i + P].bitcast(lfmt),
@@ -156,11 +177,11 @@ def tile_attributegnn_pb_v_kernel(tc, attr_rep, bwd_proj, self_weighted, proj, g
             return accs
 
         def t3(u):
-            st[("a1", u)] = mms(st[("x", u)], E4, st[("b", u)], E5, ["acc"] * 4)
+            st[("a1", u)] = mms(st[("x", u)], E4, st[("b", u)], E5, ["acc"] * 4, st[("pre", u)])
 
         def t4(u):
             tags = ["acc"] * 4 if u < A - 1 else ["tw", "tw", "td", "td"]
-            st[("a0", u)] = mms(st[("d", u)], E5, st[("w", u)], E4, tags)
+            st[("a0", u)] = mms(st[("d", u)], E5, st[("w", u)], E4, tags, None)
 
         def s3(u):
             o1 = sb.tile([P, 4, W], F32, name="o1", tag="mid", bufs=10)
@@ -203,6 +224,7 @@ def tile_attributegnn_pb_v_kernel(tc, attr_rep, bwd_proj, self_weighted, proj, g
             t2(u)
             if u + 1 < A:
                 t1(u + 1)
+            keep_warm(u)
             s2(u)
             if u + 1 < A:
                 s1(u + 1)

@@ -16,7 +16,6 @@ ALU = mybir.AluOpType
 P = 128
 A = 8
 W = 512
-NWARM = 6
 
 
 def tile_attributegnn_pb_v_kernel(tc, attr_rep, bwd_proj, self_weighted, proj, grad_out, out_0, out_1):
@@ -27,7 +26,7 @@ def tile_attributegnn_pb_v_kernel(tc, attr_rep, bwd_proj, self_weighted, proj, g
     g_v = grad_out.rearrange("(p j) w -> p j w", j=4)
     w_v = bwd_proj.rearrange("a (m t) p -> m a t p", t=4)
     o0_v = out_0.rearrange("(m j) a r -> m j a r", j=4)
-    o1_v = out_1.rearrange("a (m t) p -> m a t p", t=4)
+    o1_v = out_1.rearrange("a (t m) p -> m a t p", t=4)
 
     with ExitStack() as ctx:
         const = ctx.enter_context(tc.tile_pool(name="const", bufs=1))
@@ -57,7 +56,7 @@ def tile_attributegnn_pb_v_kernel(tc, attr_rep, bwd_proj, self_weighted, proj, g
         ident = const.tile([P, P], F32, name="ident")
         sw_sb = const.tile([P, 32], F32, name="sw_sb")
         g_sb = const.tile([P, 4, W], BF16, name="g_sb")
-        nc.vector.memset(zrow[:], 0.0)
+        nc.gpsimd.memset(zrow[:], 0.0)
         nc.vector.memset(ones[:], 1.0)
         nc.sync.dma_start(out=zrow[0:1, 0:A], in_=self_weighted.rearrange("o a i -> o (a i)"))
         alloc_pair(0)
@@ -117,14 +116,17 @@ def tile_attributegnn_pb_v_kernel(tc, attr_rep, bwd_proj, self_weighted, proj, g
 
         def v3(u):
             dzb = sb.tile([P, W, 4], BF16, name="dzb", tag="dzb", bufs=2, align_bytes=64)
-            nc.vector.tensor_copy(out=dzb[:], in_=st[("dz", u)][:].rearrange("p j w -> p w j"))
+            nc.vector.tensor_copy(
+                out=dzb[:].rearrange("p (c i) j -> p c j i", i=4),
+                in_=st[("dz", u)][:].rearrange("p j (c i) -> p c j i", i=4),
+            )
             st[("dzb", u)] = dzb
 
         def v4(u):
             xg = sb.tile([P, W, 4], BF16, name="xg", tag="xg", bufs=2, align_bytes=64)
             nc.vector.tensor_copy(
-                out=xg[:].rearrange("p (t m) j -> p t m j", t=4),
-                in_=xt[u // 2][:, :, u % 2, :].rearrange("p j (m t) -> p t m j", t=4),
+                out=xg[:].rearrange("p (c i) j -> p c j i", i=4),
+                in_=xt[u // 2][:, :, u % 2, :].rearrange("p j (c i) -> p c j i", i=4),
             )
             st[("xg", u)] = xg
 
@@ -140,30 +142,10 @@ def tile_attributegnn_pb_v_kernel(tc, attr_rep, bwd_proj, self_weighted, proj, g
         def s2(u):
             st[("dg", u)] = regroup(st[("db", u)], "dg")
 
-        def keep_warm(u):
+        def mms(lhs, lfmt, rhs, rfmt, tags):
             accs = []
             for i in range(4):
-                acc = psum.tile([P, W], F32, name="acc", tag="acc", bufs=4)
-                accs.append(acc)
-            for i in range(NWARM if u > 0 else 0):
-                nc.tensor.matmul_mx(
-                    out=accs[i % 4][:],
-                    lhsT=st[("d", u - 1)][0][:, 0:P].bitcast(E5),
-                    lhsT_scale=st[("d", u - 1)][1][:, 0:P],
-                    rhs=st[("w", u - 1)][0][:].bitcast(E4),
-                    rhs_scale=st[("w", u - 1)][1][:],
-                    start=True,
-                    stop=True,
-                )
-            st[("pre", u)] = accs
-
-        def mms(lhs, lfmt, rhs, rfmt, tags, pre):
-            accs = []
-            for i in range(4):
-                if pre is None:
-                    acc = psum.tile([P, W], F32, name=tags[i], tag=tags[i], bufs=(4 if tags[i] == "acc" else 2))
-                else:
-                    acc = pre[i]
+                acc = psum.tile([P, W], F32, name=tags[i], tag=tags[i], bufs=(4 if tags[i] == "acc" else 2))
                 nc.tensor.matmul_mx(
                     out=acc[:],
                     lhsT=lhs[0][:, P * i : P * i + P].bitcast(lfmt),
@@ -177,36 +159,41 @@ def tile_attributegnn_pb_v_kernel(tc, attr_rep, bwd_proj, self_weighted, proj, g
             return accs
 
         def t3(u):
-            st[("a1", u)] = mms(st[("x", u)], E4, st[("b", u)], E5, ["acc"] * 4, st[("pre", u)])
+            st[("a1", u)] = mms(st[("x", u)], E4, st[("b", u)], E5, ["acc"] * 4)
 
         def t4(u):
             tags = ["acc"] * 4 if u < A - 1 else ["tw", "tw", "td", "td"]
-            st[("a0", u)] = mms(st[("d", u)], E5, st[("w", u)], E4, tags, None)
+            st[("a0", u)] = mms(st[("d", u)], E5, st[("w", u)], E4, tags)
 
         def s3(u):
             o1 = sb.tile([P, 4, W], F32, name="o1", tag="mid", bufs=10)
             last = u == A - 1
             for i in range(4):
-                nc.scalar.copy(out=o1[:, i, :], in_=st[("a1", u)][i][:])
+                if last and i < 3:
+                    nc.vector.tensor_copy(out=o1[:, i, :], in_=st[("a1", u)][i][:])
+                else:
+                    nc.scalar.copy(out=o1[:, i, :], in_=st[("a1", u)][i][:])
                 if last and i % 2 == 1:
                     nc.sync.dma_start(out=o1_v[:, u, i - 1 : i + 1], in_=o1[:, i - 1 : i + 1, :])
             if not last:
                 nc.sync.dma_start(out=o1_v[:, u], in_=o1[:])
 
         def s4(u):
-            if u % 2 == 0:
-                st[("o0", u // 2)] = sb.tile([P, 4, 2, W], F32, name="o0", tag="big", bufs=5)
-            o0 = st[("o0", u // 2)]
             last = u == A - 1
+            single = u >= A - 2
+            if single:
+                o0 = sb.tile([P, 4, 1, W], F32, name="o0s", tag="mid", bufs=10)
+            elif u % 2 == 0:
+                o0 = sb.tile([P, 4, 2, W], F32, name="o0", tag="big", bufs=5)
+                st[("o0", u // 2)] = o0
+            else:
+                o0 = st[("o0", u // 2)]
             for j in range(4):
-                dst = o0[:, j, u % 2, :].rearrange("p (m t) -> p m t", t=4)
+                dst = o0[:, j, 0 if single else u % 2, :].rearrange("p (m t) -> p m t", t=4)
                 src = st[("a0", u)][j][:].rearrange("p (t m) -> p m t", t=4)
-                if last:
-                    nc.vector.tensor_copy(out=dst, in_=src)
-                    if j % 2 == 1:
-                        nc.sync.dma_start(out=o0_v[:, j - 1 : j + 1, u, :], in_=o0[:, j - 1 : j + 1, 1, :])
-                else:
-                    nc.scalar.copy(out=dst, in_=src)
+                nc.scalar.copy(out=dst, in_=src)
+                if last and j % 2 == 1:
+                    nc.sync.dma_start(out=o0_v[:, j - 1 : j + 1, u, :], in_=o0[:, j - 1 : j + 1, 0, :])
             if u == A - 2:
                 nc.sync.dma_start(out=o0_v[:, :, u, :], in_=o0[:, :, 0, :])
             elif u % 2 == 1 and not last:
@@ -224,17 +211,17 @@ def tile_attributegnn_pb_v_kernel(tc, attr_rep, bwd_proj, self_weighted, proj, g
             t2(u)
             if u + 1 < A:
                 t1(u + 1)
-            keep_warm(u)
             s2(u)
             if u + 1 < A:
                 s1(u + 1)
             v4(u)
             v3(u)
             quant(st[("wg", u)], E4, "w", u)
+            if u == A - 1:
+                quant(st[("dg", u)], E5, "d", u)
+                t4(u)
+                s4(u)
             quant(st[("xg", u)], E4, "x", u)
             quant(st[("dzb", u)], E5, "b", u)
             t3(u)
             s3(u)
-        quant(st[("dg", A - 1)], E5, "d", A - 1)
-        t4(A - 1)
-        s4(A - 1)

@@ -26,7 +26,7 @@ def tile_attributegnn_pb_v_kernel(tc, attr_rep, bwd_proj, self_weighted, proj, g
     g_v = grad_out.rearrange("(p j) w -> p j w", j=4)
     w_v = bwd_proj.rearrange("a (m t) p -> m a t p", t=4)
     o0_v = out_0.rearrange("(m j) a r -> m j a r", j=4)
-    o1_v = out_1.rearrange("a (t m) p -> m a t p", t=4)
+    o1_v = out_1.rearrange("a (m t) p -> m a t p", t=4)
 
     with ExitStack() as ctx:
         const = ctx.enter_context(tc.tile_pool(name="const", bufs=1))
@@ -125,8 +125,8 @@ def tile_attributegnn_pb_v_kernel(tc, attr_rep, bwd_proj, self_weighted, proj, g
         def v4(u):
             xg = sb.tile([P, W, 4], BF16, name="xg", tag="xg", bufs=2, align_bytes=64)
             nc.vector.tensor_copy(
-                out=xg[:].rearrange("p (c i) j -> p c j i", i=4),
-                in_=xt[u // 2][:, :, u % 2, :].rearrange("p j (c i) -> p c j i", i=4),
+                out=xg[:].rearrange("p (t m) j -> p t m j", t=4),
+                in_=xt[u // 2][:, :, u % 2, :].rearrange("p j (m t) -> p t m j", t=4),
             )
             st[("xg", u)] = xg
 

from contextlib import ExitStack

import concourse.mybir as mybir
from concourse.masks import make_identity

FLOPS = 2 * 2 * 8 * 512 * 512 * 512

F32 = mybir.dt.float32
BF16 = mybir.dt.bfloat16
U32 = mybir.dt.uint32
U8 = mybir.dt.uint8
E4 = mybir.dt.float8_e4m3fn_x4
E5 = mybir.dt.float8_e5m2_x4
ALU = mybir.AluOpType

P = 128
A = 8
W = 512


def tile_attributegnn_pb_v_kernel(tc, attr_rep, bwd_proj, self_weighted, proj, grad_out, out_0, out_1):
    nc = tc.nc

    proj_v = proj.rearrange("(p j) a w -> p j a w", j=4)
    x_v = attr_rep.rearrange("(p j) a r -> p j a r", j=4)
    g_v = grad_out.rearrange("(p j) w -> p j w", j=4)
    w_v = bwd_proj.rearrange("a (m t) p -> m a t p", t=4)
    o0_v = out_0.rearrange("(m j) a r -> m j a r", j=4)
    o1_v = out_1.rearrange("a (m t) p -> m a t p", t=4)

    with ExitStack() as ctx:
        const = ctx.enter_context(tc.tile_pool(name="const", bufs=1))
        sb = ctx.enter_context(tc.tile_pool(name="sb", bufs=2))
        psum = ctx.enter_context(tc.psum_pool(name="psum", bufs=2))
        ctx.enter_context(tc.manual_schedule())

        pt = {}
        xt = {}
        wt = {}
        st = {}

        def alloc_pair(k):
            pt[k] = sb.tile([P, 4, 2, W], F32, name="pt", tag="big", bufs=5)
            xt[k] = sb.tile([P, 4, 2, W], BF16, name="xt", tag="mid", bufs=10)
            wt[k] = sb.tile([P, 2, 4, W], BF16, name="wt", tag="mid", bufs=10)

        def load_pair(k):
            alloc_pair(k)
            nc.sync.dma_start(out=pt[k][:], in_=proj_v[:, :, 2 * k : 2 * k + 2, :])
            nc.sync.dma_start(out=wt[k][:], in_=w_v[:, 2 * k : 2 * k + 2])
            nc.sync.dma_start(out=xt[k][:], in_=x_v[:, :, 2 * k : 2 * k + 2, :])

        zrow = const.tile([P, 32], BF16, name="zrow")
        ones = const.tile([P, P], BF16, name="ones")
        warm = const.tile([P, 1], BF16, name="warm")
        ident = const.tile([P, P], F32, name="ident")
        sw_sb = const.tile([P, 32], F32, name="sw_sb")
        g_sb = const.tile([P, 4, W], BF16, name="g_sb")
        nc.gpsimd.memset(zrow[:], 0.0)
        nc.vector.memset(ones[:], 1.0)
        nc.sync.dma_start(out=zrow[0:1, 0:A], in_=self_weighted.rearrange("o a i -> o (a i)"))
        alloc_pair(0)
        nc.sync.dma_start(out=pt[0][:, :, 0, :], in_=proj_v[:, :, 0, :])
        nc.sync.dma_start(out=g_sb[:], in_=g_v)
        nc.sync.dma_start(out=xt[0][:, :, 0, :], in_=x_v[:, :, 0, :])
        nc.sync.dma_start(out=wt[0][:, 0], in_=w_v[:, 0])
        nc.sync.dma_start(out=pt[0][:, :, 1, :], in_=proj_v[:, :, 1, :])
        nc.sync.dma_start(out=xt[0][:, :, 1, :], in_=x_v[:, :, 1, :])
        nc.sync.dma_start(out=wt[0][:, 1], in_=w_v[:, 1])
        load_pair(1)
        load_pair(2)
        load_pair(3)
        nc.scalar.copy(out=warm[:], in_=ones[:, 0:1])
        make_identity(nc, ident[:])
        sw_ps = psum.tile([P, W], F32, name="sw_ps", tag="tw", bufs=2)
        nc.tensor.matmul(out=sw_ps[:, 0:32], lhsT=ones[:], rhs=zrow[:], start=True, stop=True)
        nc.vector.tensor_copy(out=sw_sb[:], in_=sw_ps[:, 0:32])

        def quant(src, fmt, key, u):
            codes = sb.tile([P, W], U32, name=key + "c", tag=key + "c", bufs=2, align_bytes=64)
            scales = sb.tile([P, W], U8, name=key + "s", tag=key + "s", bufs=2, align_bytes=64)
            nc.vector.quantize_mx(out=codes[:].bitcast(fmt), scales=scales[:], in_=src[:].rearrange("p c k -> p (c k)"))
            st[(key, u)] = (codes, scales)

        def transposes(words, tag):
            banks = []
            for h in range(2):
                bank = psum.tile([P, W], F32, name=tag, tag=tag, bufs=2)
                bv = bank[:].rearrange("p (e n) -> p e n", e=2)
                for s in range(2):
                    blk = 2 * h + s
                    for e in range(2):
                        nc.tensor.transpose(bv[:, e, P * s : P * s + P], words[:, 256 * blk + e : 256 * (blk + 1) : 2], ident[:])
                banks.append(bank)
            return banks

        def regroup(banks, tag):
            grouped = sb.tile([P, W, 4], BF16, name=tag, tag=tag, bufs=2, align_bytes=64)
            gw = grouped[:].rearrange("p n k -> p (n k)").bitcast(F32)
            for h in range(2):
                nc.scalar.copy(
                    out=gw[:, 512 * h : 512 * h + 512].rearrange("p (n e) -> p n e", e=2),
                    in_=banks[h][:].rearrange("p (e n) -> p n e", e=2),
                )
            return grouped

        def v1(u):
            msw = sb.tile([P, 4, W], BF16, name="msw", tag="msw", bufs=2)
            nc.vector.tensor_scalar(out=msw[:], in0=pt[u // 2][:, :, u % 2, :], scalar1=0.0, scalar2=sw_sb[:, u : u + 1], op0=ALU.is_gt, op1=ALU.mult)
            st[("msw", u)] = msw

        def v2(u):
            dz = sb.tile([P, 4, W], BF16, name="dz", tag="dz", bufs=2)
            nc.vector.tensor_tensor(out=dz[:], in0=st[("msw", u)][:], in1=g_sb[:], op=ALU.mult)
            st[("dz", u)] = dz

        def v3(u):
            dzb = sb.tile([P, W, 4], BF16, name="dzb", tag="dzb", bufs=2, align_bytes=64)
            nc.vector.tensor_copy(
                out=dzb[:].rearrange("p (c i) j -> p c j i", i=4),
                in_=st[("dz", u)][:].rearrange("p j (c i) -> p c j i", i=4),
            )
            st[("dzb", u)] = dzb

        def v4(u):
            xg = sb.tile([P, W, 4], BF16, name="xg", tag="xg", bufs=2, align_bytes=64)
            nc.vector.tensor_copy(
                out=xg[:].rearrange("p (t m) j -> p t m j", t=4),
                in_=xt[u // 2][:, :, u % 2, :].rearrange("p j (m t) -> p t m j", t=4),
            )
            st[("xg", u)] = xg

        def t1(u):
            st[("wb", u)] = transposes(wt[u // 2][:, u % 2].rearrange("p t w -> p (t w)").bitcast(F32), "tw")

        def s1(u):
            st[("wg", u)] = regroup(st[("wb", u)], "wg")

        def t2(u):
            st[("db", u)] = transposes(st[("dz", u)][:].rearrange("p j w -> p (j w)").bitcast(F32), "td")

        def s2(u):
            st[("dg", u)] = regroup(st[("db", u)], "dg")

        def mms(lhs, lfmt, rhs, rfmt, tags):
            accs = []
            for i in range(4):
                acc = psum.tile([P, W], F32, name=tags[i], tag=tags[i], bufs=(4 if tags[i] == "acc" else 2))
                nc.tensor.matmul_mx(
                    out=acc[:],
                    lhsT=lhs[0][:, P * i : P * i + P].bitcast(lfmt),
                    lhsT_scale=lhs[1][:, P * i : P * i + P],
                    rhs=rhs[0][:].bitcast(rfmt),
                    rhs_scale=rhs[1][:],
                    start=True,
                    stop=True,
                )
                accs.append(acc)
            return accs

        def t3(u):
            st[("a1", u)] = mms(st[("x", u)], E4, st[("b", u)], E5, ["acc"] * 4)

        def t4(u):
            tags = ["acc"] * 4 if u < A - 1 else ["tw", "tw", "td", "td"]
            st[("a0", u)] = mms(st[("d", u)], E5, st[("w", u)], E4, tags)

        def s3(u):
            o1 = sb.tile([P, 4, W], F32, name="o1", tag="mid", bufs=10)
            last = u == A - 1
            for i in range(4):
                if last and i < 3:
                    nc.vector.tensor_copy(out=o1[:, i, :], in_=st[("a1", u)][i][:])
                else:
                    nc.scalar.copy(out=o1[:, i, :], in_=st[("a1", u)][i][:])
                if last and i % 2 == 1:
                    nc.sync.dma_start(out=o1_v[:, u, i - 1 : i + 1], in_=o1[:, i - 1 : i + 1, :])
            if not last:
                nc.sync.dma_start(out=o1_v[:, u], in_=o1[:])

        def s4(u):
            last = u == A - 1
            single = u >= A - 2
            if single:
                o0 = sb.tile([P, 4, 1, W], F32, name="o0s", tag="mid", bufs=10)
            elif u % 2 == 0:
                o0 = sb.tile([P, 4, 2, W], F32, name="o0", tag="big", bufs=5)
                st[("o0", u // 2)] = o0
            else:
                o0 = st[("o0", u // 2)]
            for j in range(4):
                dst = o0[:, j, 0 if single else u % 2, :].rearrange("p (m t) -> p m t", t=4)
                src = st[("a0", u)][j][:].rearrange("p (t m) -> p m t", t=4)
                nc.scalar.copy(out=dst, in_=src)
                if last and j % 2 == 1:
                    nc.sync.dma_start(out=o0_v[:, j - 1 : j + 1, u, :], in_=o0[:, j - 1 : j + 1, 0, :])
            if u == A - 2:
                nc.sync.dma_start(out=o0_v[:, :, u, :], in_=o0[:, :, 0, :])
            elif u % 2 == 1 and not last:
                nc.sync.dma_start(out=o0_v[:, :, u - 1 : u + 1, :], in_=o0[:])

        t1(0)
        s1(0)
        for u in range(A):
            v1(u)
            if u > 0:
                quant(st[("dg", u - 1)], E5, "d", u - 1)
                t4(u - 1)
                s4(u - 1)
            v2(u)
            t2(u)
            if u + 1 < A:
                t1(u + 1)
            s2(u)
            if u + 1 < A:
                s1(u + 1)
            v4(u)
            v3(u)
            quant(st[("wg", u)], E4, "w", u)
            if u == A - 1:
                quant(st[("dg", u)], E5, "d", u)
                t4(u)
                s4(u)
            quant(st[("xg", u)], E4, "x", u)
            quant(st[("dzb", u)], E5, "b", u)
            t3(u)
            s3(u)
